import numpy as np
import ml_dtypes


def mxq(x, axis, fmt="e4m3"):
    dtype, down = {"e4m3": (ml_dtypes.float8_e4m3fn, 7), "e5m2": (ml_dtypes.float8_e5m2, 14)}[fmt]
    v = np.moveaxis(np.asarray(x, np.float32).astype(ml_dtypes.bfloat16).astype(np.float64), axis, -1)
    blocks = v.reshape(v.shape[:-1] + (-1, 32))
    amax = np.abs(blocks).max(-1, keepdims=True)
    byte = np.maximum(np.where(amax > 0, np.frexp(amax)[1] - 1 + 127, 0) - down, 1)
    scale = np.exp2(byte - 127.0)
    codes = (blocks / scale).astype(np.float32).astype(dtype).astype(np.float64)
    return np.moveaxis((codes * scale).reshape(v.shape), -1, axis)


WIDE = False


def mx_kscale(k):
    if not WIDE:
        return np.ones(k)
    levels = np.array([10, -10, 5, -5, 0])
    if k % 512:
        return np.exp2(np.random.permutation(np.resize(levels, k // 32))).repeat(32)
    a = np.empty((k // 512, 16))
    for p in range(k // 512):
        a[p, :8] = np.random.permutation(np.resize(levels, 8))
        for g in range(8):
            far = levels[np.abs(levels - a[p, g]) >= 10]
            a[p, g + 8] = far[np.random.randint(len(far))]
    return np.exp2(a.ravel()).repeat(32)


BF16 = ml_dtypes.bfloat16


def bf(x):
    return np.asarray(x, np.float32).astype(BF16)


def f64(x):
    return np.asarray(x).astype(np.float64)


B, H, C, W = 2, 64, 1024, 512
EPS = 1e-8
MASK_MIN = 0.0


def setup_inputs():
    s = mx_kscale(W)
    rows = 0.5 + 1.5 * np.random.random_sample((B, C, 1))
    return {"memory": bf(np.random.standard_normal((B, C, W)) * rows * s),
            "keys": bf(np.random.standard_normal((B, H, W)) * s),
            "betas": bf(np.sqrt(W) * (0.6 + 0.6 * np.random.random_sample((B, H)))),
            "mask": bf(np.random.random_sample((B, H, W)) / s)}


def reference(memory, keys, betas, mask):
    memory, keys, betas = f64(memory), f64(keys), f64(betas)
    mask = f64(mask) * (1.0 - MASK_MIN) + MASK_MIN
    m2 = mask * mask
    keys_m = keys * mask
    dots = mxq(keys * m2, 2, "e4m3") @ mxq(memory, 2, "e4m3").transpose(0, 2, 1)
    keys_norm = np.sqrt((keys_m * keys_m).sum(-1))
    mem_norm = np.sqrt(mxq(m2, 2, "e4m3") @ mxq(memory * memory, 2, "e4m3").transpose(0, 2, 1))
    norm = keys_norm[..., None] * mem_norm
    scores = dots / (norm + EPS) * betas[..., None]
    e = np.exp(scores - scores.max(-1, keepdims=True))
    return e / e.sum(-1, keepdims=True)

@@ -1,0 +1,223 @@
+from contextlib import ExitStack
+
+import concourse.mybir as mybir
+from concourse.masks import make_identity
+
+F32 = mybir.dt.float32
+BF16 = mybir.dt.bfloat16
+I32 = mybir.dt.int32
+U32 = mybir.dt.uint32
+U8 = mybir.dt.uint8
+FP8X4 = mybir.dt.float8_e4m3fn_x4
+ACT = mybir.ActivationFunctionType
+ALU = mybir.AluOpType
+AXIS = mybir.AxisListType
+
+B, H, C, W = 2, 64, 1024, 512
+P = 128
+PACK = 4
+EPS = 1e-8
+GUARD = 1e-26
+
+T = 2
+CELLS = T * P
+CHUNKS = C // CELLS
+LAST = CHUNKS - 1
+TURN_AHEAD = 2
+VECTOR_COLS = 640
+
+FLOPS = 2 * 2 * B * H * C * W
+
+assert B * H == P and W == P * PACK
+
+
+def tile_contentaddressing_s_kernel(tc, memory, keys, betas, mask, out):
+    nc = tc.nc
+    with ExitStack() as stack:
+        const = stack.enter_context(tc.tile_pool(name="const", bufs=1))
+        chunk = stack.enter_context(tc.tile_pool(name="chunk", bufs=CHUNKS))
+        flip = stack.enter_context(tc.psum_pool(name="flip", bufs=2 * TURN_AHEAD))
+        sums = stack.enter_context(tc.psum_pool(name="sums", bufs=CHUNKS))
+        stack.enter_context(tc.manual_schedule())
+
+        beta_bf = const.tile([P, 1], BF16)
+        with nc.allow_non_contiguous_dma(reason="one beta for each partition, 128 in all"):
+            nc.scalar.dma_start(out=beta_bf[:], in_=betas.rearrange("b (h o) -> (b h) o", o=1))
+
+        ident = const.tile([P, P], F32)
+        make_identity(nc, ident[:])
+        guard = const.tile([P, 1], F32)
+        nc.vector.memset(guard[:], GUARD)
+        first_table = const.tile([P, 1], F32)
+        nc.scalar.activation(out=first_table[:], in_=guard[:], func=ACT.Abs_reciprocal_sqrt)
+        head_vals = const.tile([P, 2 * B * 2 * H * PACK], BF16, align_bytes=64)
+        nc.vector.memset(head_vals[:].bitcast(I32), 0)
+
+        mem_view = memory.rearrange("b (q j t) w -> q j b (t w)", q=CHUNKS, j=P, t=T)
+        cells_sb = [chunk.tile([P, B, T * W], BF16, name="x") for q in range(CHUNKS)]
+        mask_sb = const.tile([P, W], BF16)
+        keys_sb = const.tile([P, W], BF16)
+        nc.sync.dma_start(out=cells_sb[0][:, 0, :], in_=mem_view[0][:, 0, :])
+        nc.sync.dma_start(out=mask_sb[:], in_=mask.rearrange("b h w -> (b h) w"))
+        nc.sync.dma_start(out=keys_sb[:], in_=keys.rearrange("b h w -> (b h) w"))
+        nc.sync.dma_start(out=cells_sb[0][:, 1, :], in_=mem_view[0][:, 1, :])
+        for q in range(1, CHUNKS):
+            nc.sync.dma_start(out=cells_sb[q][:], in_=mem_view[q])
+
+        mem_vals = [
+            chunk.tile([P, B, P, T * PACK], BF16, name="mem_vals", align_bytes=64)
+            for q in range(CHUNKS)
+        ]
+        codes = {}
+        scales = {}
+        acc = {}
+        inv_mem = const.tile([P, C], F32)
+        den_sq = const.tile([P, C], F32)
+        inv_den = const.tile([P, C], F32)
+        cosine = const.tile([P, C], F32)
+        scores = const.tile([P, C + 1], F32)
+
+        def turn(q):
+            words = cells_sb[q][:].bitcast(F32)
+            for b in range(B):
+                turned = flip.tile([P, PACK, P], F32, name="turned")
+                for m in range(T * 2):
+                    first = (m // 2) * (W // 2) + m % 2
+                    nc.tensor.transpose(
+                        turned[:, m, :], words[:, b, first : first + W // 2 - 1 : 2], ident[:]
+                    )
+                nc.scalar.copy(
+                    out=mem_vals[q][:].bitcast(F32)[:, b, :, :],
+                    in_=turned[:].rearrange("p m j -> p j m"),
+                )
+
+        def square_and_quantise(q):
+            flat = mem_vals[q][:].rearrange("p b j v -> p (b j v)")
+            sq_vals = chunk.tile([P, B * CELLS * PACK], BF16, name="sq_vals", align_bytes=64)
+            nc.vector.tensor_mul(out=sq_vals[:], in0=flat, in1=flat)
+            for o, vals in enumerate((flat, sq_vals[:])):
+                codes[q, o] = chunk.tile([P, B * CELLS], U32, name="codes%d" % o, align_bytes=64)
+                scales[q, o] = chunk.tile([P, B * CELLS], U8, name="scales%d" % o, align_bytes=64)
+                nc.vector.quantize_mx(
+                    out=codes[q, o][:].bitcast(FP8X4), scales=scales[q, o][:], in_=vals
+                )
+
+        def multiply(q):
+            acc[q] = sums.tile([P, 2, CELLS], F32, name="acc")
+            for o in range(2):
+                for b in range(B):
+                    heads = slice(o * 4 * H + b * H, o * 4 * H + b * H + P)
+                    cols = slice(b * CELLS, (b + 1) * CELLS)
+                    nc.tensor.matmul_mx(
+                        out=acc[q][:, o, :],
+                        lhsT=head_codes[:, heads].bitcast(FP8X4),
+                        lhsT_scale=head_scales[:, heads],
+                        rhs=codes[q, o][:, cols].bitcast(FP8X4),
+                        rhs_scale=scales[q, o][:, cols],
+                        start=(b == 0),
+                        stop=(b == B - 1),
+                    )
+
+        def inverse_mem_norm(q):
+            nc.scalar.activation(
+                out=inv_mem[:, q * CELLS : (q + 1) * CELLS], in_=acc[q][:, 1, :],
+                func=ACT.Abs_reciprocal_sqrt, bias=guard[:],
+            )
+
+        def score(first, stop):
+            cols = slice(first * CELLS, stop * CELLS)
+            nc.scalar.activation(
+                out=den_sq[:, cols], in_=inv_mem[:, cols], func=ACT.Square,
+                scale=EPS, bias=keys_norm[:],
+            )
+            nc.scalar.activation(
+                out=inv_den[:, cols], in_=den_sq[:, cols], func=ACT.Abs_reciprocal_sqrt
+            )
+            for q in range(first, stop):
+                own = slice(q * CELLS, (q + 1) * CELLS)
+                nc.vector.scalar_tensor_tensor(
+                    out=cosine[:, own], in0=acc[q][:, 0, :], scalar=beta[:, 0:1],
+                    in1=inv_mem[:, own], op0=ALU.mult, op1=ALU.mult,
+                )
+            nc.vector.tensor_mul(out=scores[:, cols], in0=cosine[:, cols], in1=inv_den[:, cols])
+
+        turn(0)
+
+        m2 = const.tile([P, W], F32)
+        nc.vector.tensor_mul(out=m2[:], in0=mask_sb[:], in1=mask_sb[:])
+        km2 = const.tile([P, W], F32)
+        nc.vector.tensor_mul(out=km2[:], in0=keys_sb[:], in1=m2[:])
+        km = const.tile([P, W], F32)
+        nc.vector.tensor_mul(out=km[:], in0=keys_sb[:], in1=mask_sb[:])
+
+        head_view = head_vals[:].rearrange(
+            "p (o a z h t) -> p o a z h t", o=2, a=B, z=2, h=H, t=PACK
+        )
+        for o, rows in ((1, m2), (0, km2)):
+            turned = flip.tile([P, PACK, P], F32, name="turned")
+            by_word = rows[:].rearrange("r (p t) -> r t p", t=PACK)
+            for t in range(PACK):
+                nc.tensor.transpose(turned[:, t, :], by_word[:, t, :], ident[:])
+            nc.scalar.copy(
+                out=head_view[:, o, :, 0, :, :],
+                in_=turned[:].rearrange("p t (a h) -> p a h t", a=B),
+            )
+
+        km_sq = const.tile([P, W], F32)
+        kn_sq = const.tile([P, 1], F32)
+        nc.scalar.activation(out=km_sq[:], in_=km[:], func=ACT.Square, accum_out=kn_sq[:])
+        kn_inv = const.tile([P, 1], F32)
+        nc.scalar.activation(
+            out=kn_inv[:], in_=kn_sq[:], func=ACT.Abs_reciprocal_sqrt, bias=guard[:]
+        )
+
+        turn(1)
+        square_and_quantise(0)
+        head_codes = const.tile([P, 2 * B * 2 * H], U32, align_bytes=64)
+        head_scales = const.tile([P, 2 * B * 2 * H], U8, align_bytes=64)
+        nc.vector.quantize_mx(
+            out=head_codes[:].bitcast(FP8X4), scales=head_scales[:], in_=head_vals[:]
+        )
+        keys_norm = const.tile([P, 1], F32)
+        nc.vector.reciprocal(out=keys_norm[:], in_=kn_inv[:])
+        beta = const.tile([P, 1], F32)
+        nc.vector.tensor_copy(out=beta[:], in_=beta_bf[:])
+
+        for q in range(LAST):
+            if q + TURN_AHEAD < CHUNKS:
+                turn(q + TURN_AHEAD)
+            multiply(q)
+            inverse_mem_norm(q)
+            square_and_quantise(q + 1)
+        score(0, LAST)
+        nc.vector.tensor_reduce(
+            out=scores[:, C : C + 1], in_=scores[:, 0 : LAST * CELLS], axis=AXIS.X, op=ALU.max
+        )
+        multiply(LAST)
+        inverse_mem_norm(LAST)
+        score(LAST, CHUNKS)
+        next_table = const.tile([P, 1], F32)
+        nc.scalar.activation(out=next_table[:], in_=inv_den[:, C - 1 : C], func=ACT.Exp)
+
+        neg_max = const.tile([P, 1], F32)
+        nc.vector.tensor_reduce(
+            out=neg_max[:], in_=scores[:, LAST * CELLS : C + 1], axis=AXIS.X, op=ALU.max, negate=True
+        )
+        expd = const.tile([P, C], F32)
+        total = const.tile([P, 1], F32)
+        nc.scalar.activation(
+            out=expd[:], in_=scores[:, 0:C], func=ACT.Exp, bias=neg_max[:], accum_out=total[:]
+        )
+        inv_total = const.tile([P, 1], F32)
+        nc.vector.reciprocal(out=inv_total[:], in_=total[:])
+        out_rows = out.rearrange("b h c -> (b h) c")
+        left = const.tile([P, VECTOR_COLS], F32)
+        nc.vector.tensor_scalar_mul(
+            out=left[:], in0=expd[:, 0:VECTOR_COLS], scalar1=inv_total[:, 0:1]
+        )
+        nc.sync.dma_start(out=out_rows[:, 0:VECTOR_COLS], in_=left[:])
+        right = const.tile([P, C - VECTOR_COLS], F32)
+        nc.scalar.activation(
+            out=right[:], in_=expd[:, VECTOR_COLS:C], func=ACT.Copy, scale=inv_total[:, 0:1]
+        )
+        nc.scalar.dma_start(out=out_rows[:, VECTOR_COLS:C], in_=right[:])

@@ -19,16 +19,17 @@ PACK = 4
 EPS = 1e-8
 GUARD = 1e-26
 
-T = 2
-CELLS = T * P
-CHUNKS = C // CELLS
+TILES = (1, 2, 2, 2, 1)
+CHUNKS = len(TILES)
 LAST = CHUNKS - 1
-TURN_AHEAD = 2
-VECTOR_COLS = 640
+STARTS = [P * sum(TILES[:q]) for q in range(CHUNKS)]
+GROUPS = ((0, 1, 2), (3, 4))
+SCALAR_SQUARES = {3: (1,), 4: (0, 1)}
+SPLIT = STARTS[GROUPS[1][0]]
 
 FLOPS = 2 * 2 * B * H * C * W
 
-assert B * H == P and W == P * PACK
+assert B * H == P and W == P * PACK and P * sum(TILES) == C
 
 
 def tile_contentaddressing_s_kernel(tc, memory, keys, betas, mask, out):
@@ -36,8 +37,7 @@ def tile_contentaddressing_s_kernel(tc, memory, keys, betas, mask, out):
     with ExitStack() as stack:
         const = stack.enter_context(tc.tile_pool(name="const", bufs=1))
         chunk = stack.enter_context(tc.tile_pool(name="chunk", bufs=CHUNKS))
-        flip = stack.enter_context(tc.psum_pool(name="flip", bufs=2 * TURN_AHEAD))
-        sums = stack.enter_context(tc.psum_pool(name="sums", bufs=CHUNKS))
+        psum = stack.enter_context(tc.psum_pool(name="psum", bufs=8))
         stack.enter_context(tc.manual_schedule())
 
         beta_bf = const.tile([P, 1], BF16)
@@ -53,116 +53,146 @@ def tile_contentaddressing_s_kernel(tc, memory, keys, betas, mask, out):
         head_vals = const.tile([P, 2 * B * 2 * H * PACK], BF16, align_bytes=64)
         nc.vector.memset(head_vals[:].bitcast(I32), 0)
 
-        mem_view = memory.rearrange("b (q j t) w -> q j b (t w)", q=CHUNKS, j=P, t=T)
-        cells_sb = [chunk.tile([P, B, T * W], BF16, name="x") for q in range(CHUNKS)]
+        mem_view = [
+            memory[:, STARTS[q] : STARTS[q] + P * TILES[q], :].rearrange("b (j t) w -> j b (t w)", t=TILES[q])
+            for q in range(CHUNKS)
+        ]
+        cells_sb = [chunk.tile([P, B, TILES[q] * W], BF16, name="x") for q in range(CHUNKS)]
         mask_sb = const.tile([P, W], BF16)
         keys_sb = const.tile([P, W], BF16)
-        nc.sync.dma_start(out=cells_sb[0][:, 0, :], in_=mem_view[0][:, 0, :])
         nc.sync.dma_start(out=mask_sb[:], in_=mask.rearrange("b h w -> (b h) w"))
+        nc.sync.dma_start(out=cells_sb[0][:], in_=mem_view[0])
         nc.sync.dma_start(out=keys_sb[:], in_=keys.rearrange("b h w -> (b h) w"))
-        nc.sync.dma_start(out=cells_sb[0][:, 1, :], in_=mem_view[0][:, 1, :])
         for q in range(1, CHUNKS):
             nc.sync.dma_start(out=cells_sb[q][:], in_=mem_view[q])
 
         mem_vals = [
-            chunk.tile([P, B, P, T * PACK], BF16, name="mem_vals", align_bytes=64)
+            chunk.tile([P, B, P, TILES[q] * PACK], BF16, name="mem_vals", align_bytes=64)
             for q in range(CHUNKS)
         ]
+        sq_vals = {}
         codes = {}
         scales = {}
         acc = {}
-        inv_mem = const.tile([P, C], F32)
+        norm = const.tile([P, C], F32)
         den_sq = const.tile([P, C], F32)
         inv_den = const.tile([P, C], F32)
-        cosine = const.tile([P, C], F32)
+        inv = const.tile([P, C], F32)
         scores = const.tile([P, C + 1], F32)
 
         def turn(q):
-            words = cells_sb[q][:].bitcast(F32)
-            for b in range(B):
-                turned = flip.tile([P, PACK, P], F32, name="turned")
-                for m in range(T * 2):
-                    first = (m // 2) * (W // 2) + m % 2
+            words = cells_sb[q][:].rearrange("j b k -> j (b k)").bitcast(F32)
+            vals = mem_vals[q][:].rearrange("p b j v -> p (b j v)").bitcast(F32)
+            for n in range(TILES[q]):
+                turned = psum.tile([P, PACK, P], F32, name="bank")
+                for m in range(PACK):
+                    first = (n * 2 + m // 2) * (W // 2) + m % 2
                     nc.tensor.transpose(
-                        turned[:, m, :], words[:, b, first : first + W // 2 - 1 : 2], ident[:]
+                        turned[:, m, :], words[:, first : first + W // 2 - 1 : 2], ident[:]
                     )
-                nc.scalar.copy(
-                    out=mem_vals[q][:].bitcast(F32)[:, b, :, :],
-                    in_=turned[:].rearrange("p m j -> p j m"),
-                )
-
-        def square_and_quantise(q):
-            flat = mem_vals[q][:].rearrange("p b j v -> p (b j v)")
-            sq_vals = chunk.tile([P, B * CELLS * PACK], BF16, name="sq_vals", align_bytes=64)
-            nc.vector.tensor_mul(out=sq_vals[:], in0=flat, in1=flat)
-            for o, vals in enumerate((flat, sq_vals[:])):
-                codes[q, o] = chunk.tile([P, B * CELLS], U32, name="codes%d" % o, align_bytes=64)
-                scales[q, o] = chunk.tile([P, B * CELLS], U8, name="scales%d" % o, align_bytes=64)
-                nc.vector.quantize_mx(
-                    out=codes[q, o][:].bitcast(FP8X4), scales=scales[q, o][:], in_=vals
-                )
-
-        def multiply(q):
-            acc[q] = sums.tile([P, 2, CELLS], F32, name="acc")
-            for o in range(2):
-                for b in range(B):
-                    heads = slice(o * 4 * H + b * H, o * 4 * H + b * H + P)
-                    cols = slice(b * CELLS, (b + 1) * CELLS)
-                    nc.tensor.matmul_mx(
-                        out=acc[q][:, o, :],
-                        lhsT=head_codes[:, heads].bitcast(FP8X4),
-                        lhsT_scale=head_scales[:, heads],
-                        rhs=codes[q, o][:, cols].bitcast(FP8X4),
-                        rhs_scale=scales[q, o][:, cols],
-                        start=(b == 0),
-                        stop=(b == B - 1),
+                done = vals[:, n * PACK * P : (n + 1) * PACK * P]
+                if TILES[q] == 1:
+                    nc.scalar.copy(
+                        out=done.rearrange("p (b j u) -> p b j u", b=B, u=2),
+                        in_=turned[:].rearrange("p (b u) j -> p b j u", u=2),
+                    )
+                else:
+                    nc.scalar.copy(
+                        out=done.rearrange("p (j m) -> p j m", m=PACK),
+                        in_=turned[:].rearrange("p m j -> p j m"),
                     )
 
-        def inverse_mem_norm(q):
-            nc.scalar.activation(
-                out=inv_mem[:, q * CELLS : (q + 1) * CELLS], in_=acc[q][:, 1, :],
-                func=ACT.Abs_reciprocal_sqrt, bias=guard[:],
+        def flat(q):
+            return mem_vals[q][:].rearrange("p b j v -> p (b j v)")
+
+        def square(q):
+            sq_vals[q] = chunk.tile([P, B * P * TILES[q] * PACK], BF16, name="sq_vals", align_bytes=64)
+            half = P * TILES[q] * PACK
+            by_scalar = SCALAR_SQUARES.get(q, ())
+            for b in by_scalar:
+                cols = slice(b * half, (b + 1) * half)
+                nc.scalar.activation(out=sq_vals[q][:, cols], in_=flat(q)[:, cols], func=ACT.Square)
+            cols = slice(0, half * (B - len(by_scalar)))
+            if len(by_scalar) < B:
+                nc.vector.tensor_mul(out=sq_vals[q][:, cols], in0=flat(q)[:, cols], in1=flat(q)[:, cols])
+
+        def quantise(q, o):
+            codes[q, o] = chunk.tile([P, B * P * TILES[q]], U32, name="codes%d" % o, align_bytes=64)
+            scales[q, o] = chunk.tile([P, B * P * TILES[q]], U8, name="scales%d" % o, align_bytes=64)
+            nc.vector.quantize_mx(
+                out=codes[q, o][:].bitcast(FP8X4), scales=scales[q, o][:],
+                in_=flat(q) if o == 0 else sq_vals[q][:],
             )
 
-        def score(first, stop):
-            cols = slice(first * CELLS, stop * CELLS)
-            nc.scalar.activation(
-                out=den_sq[:, cols], in_=inv_mem[:, cols], func=ACT.Square,
-                scale=EPS, bias=keys_norm[:],
-            )
-            nc.scalar.activation(
-                out=inv_den[:, cols], in_=den_sq[:, cols], func=ACT.Abs_reciprocal_sqrt
-            )
-            for q in range(first, stop):
-                own = slice(q * CELLS, (q + 1) * CELLS)
-                nc.vector.scalar_tensor_tensor(
-                    out=cosine[:, own], in0=acc[q][:, 0, :], scalar=beta[:, 0:1],
-                    in1=inv_mem[:, own], op0=ALU.mult, op1=ALU.mult,
+        def multiply(q, o):
+            cells = P * TILES[q]
+            acc[q, o] = psum.tile([P, cells], F32, name="bank")
+            for b in range(B):
+                heads = slice(o * 4 * H + b * H, o * 4 * H + b * H + P)
+                cols = slice(b * cells, (b + 1) * cells)
+                nc.tensor.matmul_mx(
+                    out=acc[q, o][:],
+                    lhsT=head_codes[:, heads].bitcast(FP8X4),
+                    lhsT_scale=head_scales[:, heads],
+                    rhs=codes[q, o][:, cols].bitcast(FP8X4),
+                    rhs_scale=scales[q, o][:, cols],
+                    start=(b == 0),
+                    stop=(b == B - 1),
                 )
-            nc.vector.tensor_mul(out=scores[:, cols], in0=cosine[:, cols], in1=inv_den[:, cols])
 
-        turn(0)
+        def own(q, stop=None):
+            return slice(STARTS[q], STARTS[q] + P * sum(TILES[q : q + 1 if stop is None else stop + 1]))
+
+        def inverse_norm(q):
+            nc.scalar.activation(
+                out=norm[:, own(q)], in_=acc[q, 1][:], func=ACT.Abs_reciprocal_sqrt, bias=guard[:]
+            )
+
+        def inverse_den(g):
+            cols = own(GROUPS[g][0], GROUPS[g][-1])
+            nc.scalar.activation(
+                out=den_sq[:, cols], in_=norm[:, cols], func=ACT.Square, scale=EPS, bias=keys_norm[:]
+            )
+            nc.scalar.activation(out=inv_den[:, cols], in_=den_sq[:, cols], func=ACT.Abs_reciprocal_sqrt)
+
+        def inverse(g):
+            cols = own(GROUPS[g][0], GROUPS[g][-1])
+            nc.vector.tensor_mul(out=inv[:, cols], in0=norm[:, cols], in1=inv_den[:, cols])
+
+        def score(q):
+            nc.vector.scalar_tensor_tensor(
+                out=scores[:, own(q)], in0=acc[q, 0][:], scalar=beta[:, 0:1],
+                in1=inv[:, own(q)], op0=ALU.mult, op1=ALU.mult,
+            )
 
         m2 = const.tile([P, W], F32)
-        nc.vector.tensor_mul(out=m2[:], in0=mask_sb[:], in1=mask_sb[:])
-        km2 = const.tile([P, W], F32)
-        nc.vector.tensor_mul(out=km2[:], in0=keys_sb[:], in1=m2[:])
+        nc.scalar.activation(out=m2[:], in_=mask_sb[:], func=ACT.Square)
+        m2_bf = const.tile([P, W], BF16)
+        nc.vector.tensor_mul(out=m2_bf[:], in0=mask_sb[:], in1=mask_sb[:])
+        km2_bf = const.tile([P, W], BF16)
+        nc.vector.tensor_mul(out=km2_bf[:], in0=keys_sb[:], in1=m2[:])
         km = const.tile([P, W], F32)
         nc.vector.tensor_mul(out=km[:], in0=keys_sb[:], in1=mask_sb[:])
 
-        head_view = head_vals[:].rearrange(
-            "p (o a z h t) -> p o a z h t", o=2, a=B, z=2, h=H, t=PACK
+        head_view = head_vals[:].bitcast(F32).rearrange(
+            "p (o a z h u) -> p o a z h u", o=2, a=B, z=2, h=H, u=2
         )
-        for o, rows in ((1, m2), (0, km2)):
-            turned = flip.tile([P, PACK, P], F32, name="turned")
-            by_word = rows[:].rearrange("r (p t) -> r t p", t=PACK)
-            for t in range(PACK):
-                nc.tensor.transpose(turned[:, t, :], by_word[:, t, :], ident[:])
+
+        def turn_heads(o, rows):
+            words = rows[:].bitcast(F32)
+            turned = psum.tile([P, 2, P], F32, name="bank")
+            for u in range(2):
+                nc.tensor.transpose(turned[:, u, :], words[:, u : u + W // 2 - 1 : 2], ident[:])
             nc.scalar.copy(
                 out=head_view[:, o, :, 0, :, :],
-                in_=turned[:].rearrange("p t (a h) -> p a h t", a=B),
+                in_=turned[:].rearrange("p u (a h) -> p a h u", a=B),
             )
 
+        turn(0)
+        turn_heads(1, m2_bf)
+        turn(1)
+        turn_heads(0, km2_bf)
+        turn(2)
         km_sq = const.tile([P, W], F32)
         kn_sq = const.tile([P, 1], F32)
         nc.scalar.activation(out=km_sq[:], in_=km[:], func=ACT.Square, accum_out=kn_sq[:])
@@ -170,54 +200,93 @@ def tile_contentaddressing_s_kernel(tc, memory, keys, betas, mask, out):
         nc.scalar.activation(
             out=kn_inv[:], in_=kn_sq[:], func=ACT.Abs_reciprocal_sqrt, bias=guard[:]
         )
-
-        turn(1)
-        square_and_quantise(0)
+        turn(3)
+        turn(4)
+        square(0)
+        quantise(0, 0)
+        quantise(0, 1)
+        square(1)
         head_codes = const.tile([P, 2 * B * 2 * H], U32, align_bytes=64)
         head_scales = const.tile([P, 2 * B * 2 * H], U8, align_bytes=64)
         nc.vector.quantize_mx(
             out=head_codes[:].bitcast(FP8X4), scales=head_scales[:], in_=head_vals[:]
         )
+        multiply(0, 1)
+        multiply(0, 0)
+        square(4)
+        square(2)
+        quantise(1, 1)
+        multiply(1, 1)
+        inverse_norm(0)
+        inverse_norm(1)
+        square(3)
         keys_norm = const.tile([P, 1], F32)
         nc.vector.reciprocal(out=keys_norm[:], in_=kn_inv[:])
         beta = const.tile([P, 1], F32)
         nc.vector.tensor_copy(out=beta[:], in_=beta_bf[:])
-
-        for q in range(LAST):
-            if q + TURN_AHEAD < CHUNKS:
-                turn(q + TURN_AHEAD)
-            multiply(q)
-            inverse_mem_norm(q)
-            square_and_quantise(q + 1)
-        score(0, LAST)
-        nc.vector.tensor_reduce(
-            out=scores[:, C : C + 1], in_=scores[:, 0 : LAST * CELLS], axis=AXIS.X, op=ALU.max
-        )
-        multiply(LAST)
-        inverse_mem_norm(LAST)
-        score(LAST, CHUNKS)
+        quantise(2, 1)
+        multiply(2, 1)
+        inverse_norm(2)
+        inverse_den(0)
+        quantise(1, 0)
+        multiply(1, 0)
+        quantise(4, 1)
+        multiply(4, 1)
+        quantise(2, 0)
+        multiply(2, 0)
+        quantise(3, 1)
+        multiply(3, 1)
+        inverse_norm(4)
+        inverse_norm(3)
+        inverse_den(1)
         next_table = const.tile([P, 1], F32)
         nc.scalar.activation(out=next_table[:], in_=inv_den[:, C - 1 : C], func=ACT.Exp)
+        quantise(3, 0)
+        multiply(3, 0)
+        quantise(4, 0)
+        inverse(0)
+        score(0)
+        multiply(4, 0)
+        score(1)
+        score(2)
+        inverse(1)
 
+        nc.vector.tensor_reduce(
+            out=scores[:, C : C + 1], in_=scores[:, 0:SPLIT], axis=AXIS.X, op=ALU.max
+        )
+        score(3)
+        neg_first = const.tile([P, 1], F32)
+        nc.vector.tensor_scalar_mul(out=neg_first[:], in0=scores[:, C : C + 1], scalar1=-1.0)
+        score(4)
         neg_max = const.tile([P, 1], F32)
         nc.vector.tensor_reduce(
-            out=neg_max[:], in_=scores[:, LAST * CELLS : C + 1], axis=AXIS.X, op=ALU.max, negate=True
+            out=neg_max[:], in_=scores[:, SPLIT : C + 1], axis=AXIS.X, op=ALU.max, negate=True
         )
         expd = const.tile([P, C], F32)
-        total = const.tile([P, 1], F32)
+        sum_first = const.tile([P, 1], F32)
         nc.scalar.activation(
-            out=expd[:], in_=scores[:, 0:C], func=ACT.Exp, bias=neg_max[:], accum_out=total[:]
+            out=expd[:, 0:SPLIT], in_=scores[:, 0:SPLIT], func=ACT.Exp, bias=neg_first[:], accum_out=sum_first[:]
+        )
+        shift = const.tile([P, 1], F32)
+        nc.scalar.activation(out=shift[:], in_=scores[:, C : C + 1], func=ACT.Exp, bias=neg_max[:])
+        sum_second = const.tile([P, 1], F32)
+        nc.scalar.activation(
+            out=expd[:, SPLIT:C], in_=scores[:, SPLIT:C], func=ACT.Exp, bias=neg_max[:], accum_out=sum_second[:]
+        )
+        total = const.tile([P, 1], F32)
+        nc.vector.scalar_tensor_tensor(
+            out=total[:], in0=sum_first[:], scalar=shift[:, 0:1], in1=sum_second[:], op0=ALU.mult, op1=ALU.add
         )
         inv_total = const.tile([P, 1], F32)
         nc.vector.reciprocal(out=inv_total[:], in_=total[:])
+        inv_first = const.tile([P, 1], F32)
+        nc.vector.tensor_mul(out=inv_first[:], in0=shift[:], in1=inv_total[:])
         out_rows = out.rearrange("b h c -> (b h) c")
-        left = const.tile([P, VECTOR_COLS], F32)
-        nc.vector.tensor_scalar_mul(
-            out=left[:], in0=expd[:, 0:VECTOR_COLS], scalar1=inv_total[:, 0:1]
-        )
-        nc.sync.dma_start(out=out_rows[:, 0:VECTOR_COLS], in_=left[:])
-        right = const.tile([P, C - VECTOR_COLS], F32)
+        left = const.tile([P, SPLIT], F32)
+        nc.vector.tensor_scalar_mul(out=left[:], in0=expd[:, 0:SPLIT], scalar1=inv_first[:, 0:1])
+        nc.sync.dma_start(out=out_rows[:, 0:SPLIT], in_=left[:])
+        right = const.tile([P, C - SPLIT], F32)
         nc.scalar.activation(
-            out=right[:], in_=expd[:, VECTOR_COLS:C], func=ACT.Copy, scale=inv_total[:, 0:1]
+            out=right[:], in_=expd[:, SPLIT:C], func=ACT.Copy, scale=inv_total[:, 0:1]
         )
-        nc.scalar.dma_start(out=out_rows[:, VECTOR_COLS:C], in_=right[:])
+        nc.scalar.dma_start(out=out_rows[:, SPLIT:C], in_=right[:])

@@ -5,7 +5,6 @@ from concourse.masks import make_identity
 
 F32 = mybir.dt.float32
 BF16 = mybir.dt.bfloat16
-I32 = mybir.dt.int32
 U32 = mybir.dt.uint32
 U8 = mybir.dt.uint8
 FP8X4 = mybir.dt.float8_e4m3fn_x4
@@ -19,13 +18,13 @@ PACK = 4
 EPS = 1e-8
 GUARD = 1e-26
 
-TILES = (1, 2, 2, 2, 1)
+TILES = (1, 1, 2, 2, 2)
 CHUNKS = len(TILES)
-LAST = CHUNKS - 1
 STARTS = [P * sum(TILES[:q]) for q in range(CHUNKS)]
 GROUPS = ((0, 1, 2), (3, 4))
-SCALAR_SQUARES = {3: (1,), 4: (0, 1)}
+SCALAR_SQUARES = ((4, 0), (4, 1))
 SPLIT = STARTS[GROUPS[1][0]]
+PIECE = 256
 
 FLOPS = 2 * 2 * B * H * C * W
 
@@ -46,92 +45,153 @@ def tile_contentaddressing_s_kernel(tc, memory, keys, betas, mask, out):
 
         ident = const.tile([P, P], F32)
         make_identity(nc, ident[:])
+        swap = const.tile([P, P], F32)
+        nc.gpsimd.tensor_copy(out=swap[:, 0:H], in_=ident[:, H:P])
+        nc.gpsimd.tensor_copy(out=swap[:, H:P], in_=ident[:, 0:H])
         guard = const.tile([P, 1], F32)
         nc.vector.memset(guard[:], GUARD)
+        eps_sq = const.tile([P, 1], F32)
+        nc.vector.tensor_scalar(
+            out=eps_sq[:], in0=guard[:], scalar1=0.0, scalar2=EPS * EPS, op0=ALU.mult, op1=ALU.add
+        )
         first_table = const.tile([P, 1], F32)
         nc.scalar.activation(out=first_table[:], in_=guard[:], func=ACT.Abs_reciprocal_sqrt)
-        head_vals = const.tile([P, 2 * B * 2 * H * PACK], BF16, align_bytes=64)
-        nc.vector.memset(head_vals[:].bitcast(I32), 0)
+
+        head_codes = const.tile([P, 7 * H], U32, align_bytes=64)
+        head_scales = const.tile([P, 7 * H], U8, align_bytes=64)
+        nc.vector.memset(head_codes[:], 0)
+        nc.vector.memset(head_scales[:].bitcast(U32), 0)
 
         mem_view = [
             memory[:, STARTS[q] : STARTS[q] + P * TILES[q], :].rearrange("b (j t) w -> j b (t w)", t=TILES[q])
             for q in range(CHUNKS)
         ]
-        cells_sb = [chunk.tile([P, B, TILES[q] * W], BF16, name="x") for q in range(CHUNKS)]
+        cells_sb = [chunk.tile([P, B, TILES[q] * W], BF16, name="cells") for q in range(CHUNKS)]
         mask_sb = const.tile([P, W], BF16)
         keys_sb = const.tile([P, W], BF16)
-        nc.sync.dma_start(out=mask_sb[:], in_=mask.rearrange("b h w -> (b h) w"))
-        nc.sync.dma_start(out=cells_sb[0][:], in_=mem_view[0])
-        nc.sync.dma_start(out=keys_sb[:], in_=keys.rearrange("b h w -> (b h) w"))
-        for q in range(1, CHUNKS):
+
+        def load_mask():
+            nc.sync.dma_start(out=mask_sb[:], in_=mask.rearrange("b h w -> (b h) w"))
+
+        def load_keys():
+            nc.sync.dma_start(out=keys_sb[:], in_=keys.rearrange("b h w -> (b h) w"))
+
+        def load(q, b):
+            nc.sync.dma_start(out=cells_sb[q][:, b, :], in_=mem_view[q][:, b, :])
+
+        def load_both(q):
             nc.sync.dma_start(out=cells_sb[q][:], in_=mem_view[q])
 
+        load(0, 0)
+        load_mask()
+        load_keys()
+        load(0, 1)
+        load_both(1)
+        load_both(2)
+        load_both(3)
+        load_both(4)
+
         mem_vals = [
-            chunk.tile([P, B, P, TILES[q] * PACK], BF16, name="mem_vals", align_bytes=64)
+            chunk.tile([P, B, P * TILES[q] * PACK], BF16, name="mem_vals", align_bytes=64)
             for q in range(CHUNKS)
         ]
-        sq_vals = {}
+        sq_vals = [
+            chunk.tile([P, B, P * TILES[q] * PACK], BF16, name="sq_vals", align_bytes=64)
+            for q in range(CHUNKS)
+        ]
         codes = {}
         scales = {}
         acc = {}
-        norm = const.tile([P, C], F32)
+        m2 = const.tile([P, W], F32)
+        m2_bf = const.tile([P, W], BF16)
+        km = const.tile([P, W], F32)
+        km2_bf = const.tile([P, W], BF16)
+        km_sq = const.tile([P, W], F32)
+        kn_sq = const.tile([P, 1], F32)
+        kn_scale = const.tile([P, 1], F32)
+        beta_neg = const.tile([P, 1], F32)
+        head_vals = const.tile([P, 2, 2 * H * PACK], BF16, align_bytes=64)
+        inv_norm = const.tile([P, C], F32)
         den_sq = const.tile([P, C], F32)
         inv_den = const.tile([P, C], F32)
-        inv = const.tile([P, C], F32)
         scores = const.tile([P, C + 1], F32)
+        low = const.tile([P, 1], F32)
+        next_table = const.tile([P, 1], F32)
+        expd = const.tile([P, C], F32)
+        sum_first = const.tile([P, 1], F32)
+        sum_second = const.tile([P, 1], F32)
+        shift = const.tile([P, 1], F32)
+        total = const.tile([P, 1], F32)
+        inv_total = const.tile([P, 1], F32)
+        result = const.tile([P, C], F32)
 
-        def turn(q):
-            words = cells_sb[q][:].rearrange("j b k -> j (b k)").bitcast(F32)
-            vals = mem_vals[q][:].rearrange("p b j v -> p (b j v)").bitcast(F32)
-            for n in range(TILES[q]):
-                turned = psum.tile([P, PACK, P], F32, name="bank")
-                for m in range(PACK):
-                    first = (n * 2 + m // 2) * (W // 2) + m % 2
+        def turn(q, b):
+            words = cells_sb[q][:, b, :].bitcast(F32)
+            turned = psum.tile([P, 2 * TILES[q], P], F32, name="bank")
+            for t in range(TILES[q]):
+                for u in range(2):
+                    first = t * (W // 2) + u
                     nc.tensor.transpose(
-                        turned[:, m, :], words[:, first : first + W // 2 - 1 : 2], ident[:]
+                        turned[:, 2 * t + u, :], words[:, first : first + W // 2 - 1 : 2], ident[:]
                     )
-                done = vals[:, n * PACK * P : (n + 1) * PACK * P]
-                if TILES[q] == 1:
-                    nc.scalar.copy(
-                        out=done.rearrange("p (b j u) -> p b j u", b=B, u=2),
-                        in_=turned[:].rearrange("p (b u) j -> p b j u", u=2),
-                    )
-                else:
-                    nc.scalar.copy(
-                        out=done.rearrange("p (j m) -> p j m", m=PACK),
-                        in_=turned[:].rearrange("p m j -> p j m"),
-                    )
+            nc.scalar.copy(
+                out=mem_vals[q][:, b, :].bitcast(F32).rearrange("p (j m) -> p j m", m=2 * TILES[q]),
+                in_=turned[:].rearrange("p m j -> p j m"),
+            )
 
-        def flat(q):
-            return mem_vals[q][:].rearrange("p b j v -> p (b j v)")
+        def turn_heads(o, rows):
+            words = rows[:].bitcast(F32)
+            turned = psum.tile([P, 2, P], F32, name="bank")
+            for u in range(2):
+                nc.tensor.transpose(turned[:, u, :], words[:, u : u + W // 2 - 1 : 2], swap[:])
+            nc.scalar.copy(
+                out=head_vals[:, o, :].bitcast(F32).rearrange("p (r u) -> p r u", u=2),
+                in_=turned[:].rearrange("p u r -> p r u"),
+            )
 
-        def square(q):
-            sq_vals[q] = chunk.tile([P, B * P * TILES[q] * PACK], BF16, name="sq_vals", align_bytes=64)
-            half = P * TILES[q] * PACK
-            by_scalar = SCALAR_SQUARES.get(q, ())
-            for b in by_scalar:
-                cols = slice(b * half, (b + 1) * half)
-                nc.scalar.activation(out=sq_vals[q][:, cols], in_=flat(q)[:, cols], func=ACT.Square)
-            cols = slice(0, half * (B - len(by_scalar)))
-            if len(by_scalar) < B:
-                nc.vector.tensor_mul(out=sq_vals[q][:, cols], in0=flat(q)[:, cols], in1=flat(q)[:, cols])
+        def quantise_heads(o):
+            cols = slice(H, 3 * H) if o == 1 else slice(4 * H, 6 * H)
+            nc.vector.quantize_mx(
+                out=head_codes[:, cols].bitcast(FP8X4), scales=head_scales[:, cols], in_=head_vals[:, o, :]
+            )
+
+        def square(q, b=None):
+            which = slice(0, B) if b is None else slice(b, b + 1)
+            vals = mem_vals[q][:, which, :].rearrange("p b v -> p (b v)")
+            squares = sq_vals[q][:, which, :].rearrange("p b v -> p (b v)")
+            if b is not None and (q, b) in SCALAR_SQUARES:
+                nc.scalar.activation(out=squares, in_=vals, func=ACT.Square)
+            else:
+                nc.vector.tensor_mul(out=squares, in0=vals, in1=vals)
 
         def quantise(q, o):
             codes[q, o] = chunk.tile([P, B * P * TILES[q]], U32, name="codes%d" % o, align_bytes=64)
             scales[q, o] = chunk.tile([P, B * P * TILES[q]], U8, name="scales%d" % o, align_bytes=64)
+            vals = sq_vals[q] if o == 1 else mem_vals[q]
             nc.vector.quantize_mx(
                 out=codes[q, o][:].bitcast(FP8X4), scales=scales[q, o][:],
-                in_=flat(q) if o == 0 else sq_vals[q][:],
+                in_=vals[:].rearrange("p b v -> p (b v)"),
             )
 
+        def group_cells(g):
+            return P * sum(TILES[q] for q in GROUPS[g])
+
+        def group(g):
+            start = STARTS[GROUPS[g][0]]
+            return slice(start, start + group_cells(g))
+
         def multiply(q, o):
+            g = [i for i in range(len(GROUPS)) if q in GROUPS[i]][0]
+            if (g, o) not in acc:
+                acc[g, o] = psum.tile([P, group_cells(g)], F32, name="bank")
+            first = STARTS[q] - STARTS[GROUPS[g][0]]
             cells = P * TILES[q]
-            acc[q, o] = psum.tile([P, cells], F32, name="bank")
+            base = 0 if o == 1 else 3 * H
             for b in range(B):
-                heads = slice(o * 4 * H + b * H, o * 4 * H + b * H + P)
+                heads = slice(base + 2 * H * (1 - b), base + 2 * H * (1 - b) + P)
                 cols = slice(b * cells, (b + 1) * cells)
                 nc.tensor.matmul_mx(
-                    out=acc[q, o][:],
+                    out=acc[g, o][:, first : first + cells],
                     lhsT=head_codes[:, heads].bitcast(FP8X4),
                     lhsT_scale=head_scales[:, heads],
                     rhs=codes[q, o][:, cols].bitcast(FP8X4),
@@ -140,153 +200,155 @@ def tile_contentaddressing_s_kernel(tc, memory, keys, betas, mask, out):
                     stop=(b == B - 1),
                 )
 
-        def own(q, stop=None):
-            return slice(STARTS[q], STARTS[q] + P * sum(TILES[q : q + 1 if stop is None else stop + 1]))
-
-        def inverse_norm(q):
+        def first_root(g):
             nc.scalar.activation(
-                out=norm[:, own(q)], in_=acc[q, 1][:], func=ACT.Abs_reciprocal_sqrt, bias=guard[:]
+                out=inv_norm[:, group(g)], in_=acc[g, 1][:], func=ACT.Abs_reciprocal_sqrt,
+                scale=kn_sq[:, 0:1], bias=guard[:],
             )
 
-        def inverse_den(g):
-            cols = own(GROUPS[g][0], GROUPS[g][-1])
-            nc.scalar.activation(
-                out=den_sq[:, cols], in_=norm[:, cols], func=ACT.Square, scale=EPS, bias=keys_norm[:]
-            )
-            nc.scalar.activation(out=inv_den[:, cols], in_=den_sq[:, cols], func=ACT.Abs_reciprocal_sqrt)
-
-        def inverse(g):
-            cols = own(GROUPS[g][0], GROUPS[g][-1])
-            nc.vector.tensor_mul(out=inv[:, cols], in0=norm[:, cols], in1=inv_den[:, cols])
-
-        def score(q):
+        def denominator(g):
             nc.vector.scalar_tensor_tensor(
-                out=scores[:, own(q)], in0=acc[q, 0][:], scalar=beta[:, 0:1],
-                in1=inv[:, own(q)], op0=ALU.mult, op1=ALU.mult,
+                out=den_sq[:, group(g)], in0=inv_norm[:, group(g)], scalar=1 / (2 * EPS),
+                in1=acc[g, 1][:], op0=ALU.add, op1=ALU.mult,
             )
 
-        m2 = const.tile([P, W], F32)
-        nc.scalar.activation(out=m2[:], in_=mask_sb[:], func=ACT.Square)
-        m2_bf = const.tile([P, W], BF16)
-        nc.vector.tensor_mul(out=m2_bf[:], in0=mask_sb[:], in1=mask_sb[:])
-        km2_bf = const.tile([P, W], BF16)
-        nc.vector.tensor_mul(out=km2_bf[:], in0=keys_sb[:], in1=m2[:])
-        km = const.tile([P, W], F32)
-        nc.vector.tensor_mul(out=km[:], in0=keys_sb[:], in1=mask_sb[:])
-
-        head_view = head_vals[:].bitcast(F32).rearrange(
-            "p (o a z h u) -> p o a z h u", o=2, a=B, z=2, h=H, u=2
-        )
-
-        def turn_heads(o, rows):
-            words = rows[:].bitcast(F32)
-            turned = psum.tile([P, 2, P], F32, name="bank")
-            for u in range(2):
-                nc.tensor.transpose(turned[:, u, :], words[:, u : u + W // 2 - 1 : 2], ident[:])
-            nc.scalar.copy(
-                out=head_view[:, o, :, 0, :, :],
-                in_=turned[:].rearrange("p u (a h) -> p a h u", a=B),
+        def second_root(g):
+            nc.scalar.activation(
+                out=inv_den[:, group(g)], in_=den_sq[:, group(g)], func=ACT.Abs_reciprocal_sqrt,
+                scale=kn_scale[:, 0:1], bias=eps_sq[:],
             )
 
-        turn(0)
+        def score(g):
+            nc.vector.scalar_tensor_tensor(
+                out=scores[:, group(g)], in0=acc[g, 0][:], scalar=beta_neg[:, 0:1],
+                in1=inv_den[:, group(g)], op0=ALU.mult, op1=ALU.mult,
+            )
+
+        def m2_round():
+            nc.vector.tensor_mul(out=m2_bf[:], in0=mask_sb[:], in1=mask_sb[:])
+
+        def m2_scalar():
+            nc.scalar.activation(out=m2[:], in_=mask_sb[:], func=ACT.Square)
+
+        def m2_vector():
+            nc.vector.tensor_mul(out=m2[:], in0=mask_sb[:], in1=mask_sb[:])
+
+        def km2_round():
+            nc.vector.tensor_mul(out=km2_bf[:], in0=keys_sb[:], in1=m2[:])
+
+        def km_make():
+            nc.vector.tensor_mul(out=km[:], in0=keys_sb[:], in1=mask_sb[:])
+
+        def keys_norm():
+            nc.scalar.activation(out=km_sq[:], in_=km[:], func=ACT.Square, accum_out=kn_sq[:])
+
+        def small():
+            nc.vector.tensor_scalar_mul(out=kn_scale[:], in0=kn_sq[:], scalar1=2 * EPS)
+            nc.vector.tensor_scalar_mul(out=beta_neg[:], in0=beta_bf[:], scalar1=-1.0)
+
+        def exp_table():
+            nc.scalar.activation(out=next_table[:], in_=inv_den[:, C - 1 : C], func=ACT.Exp)
+
+        def minimum_first():
+            nc.vector.tensor_reduce(
+                out=scores[:, C : C + 1], in_=scores[:, 0:SPLIT], axis=AXIS.X, op=ALU.min
+            )
+
+        def minimum_all():
+            nc.vector.tensor_reduce(out=low[:], in_=scores[:, SPLIT : C + 1], axis=AXIS.X, op=ALU.min)
+
+        def exp_first():
+            nc.scalar.activation(
+                out=expd[:, 0:SPLIT], in_=scores[:, 0:SPLIT], func=ACT.Exp, scale=-1.0,
+                bias=scores[:, C : C + 1], accum_out=sum_first[:],
+            )
+
+        def exp_shift():
+            nc.scalar.activation(
+                out=shift[:], in_=scores[:, C : C + 1], func=ACT.Exp, scale=-1.0, bias=low[:]
+            )
+
+        def exp_second():
+            nc.scalar.activation(
+                out=expd[:, SPLIT:C], in_=scores[:, SPLIT:C], func=ACT.Exp, scale=-1.0,
+                bias=low[:], accum_out=sum_second[:],
+            )
+
+        m2_round()
+        m2_scalar()
+        km_make()
+        turn(0, 0)
+        turn(0, 1)
         turn_heads(1, m2_bf)
-        turn(1)
+        square(0, 0)
+        km2_round()
+        square(0, 1)
+        turn(1, 0)
+        turn(1, 1)
         turn_heads(0, km2_bf)
-        turn(2)
-        km_sq = const.tile([P, W], F32)
-        kn_sq = const.tile([P, 1], F32)
-        nc.scalar.activation(out=km_sq[:], in_=km[:], func=ACT.Square, accum_out=kn_sq[:])
-        kn_inv = const.tile([P, 1], F32)
-        nc.scalar.activation(
-            out=kn_inv[:], in_=kn_sq[:], func=ACT.Abs_reciprocal_sqrt, bias=guard[:]
-        )
-        turn(3)
-        turn(4)
-        square(0)
+        keys_norm()
         quantise(0, 0)
         quantise(0, 1)
+        turn(2, 0)
+        turn(2, 1)
         square(1)
-        head_codes = const.tile([P, 2 * B * 2 * H], U32, align_bytes=64)
-        head_scales = const.tile([P, 2 * B * 2 * H], U8, align_bytes=64)
-        nc.vector.quantize_mx(
-            out=head_codes[:].bitcast(FP8X4), scales=head_scales[:], in_=head_vals[:]
-        )
+        quantise_heads(1)
+        quantise_heads(0)
+        small()
+        turn(3, 0)
+        turn(3, 1)
+        turn(4, 0)
+        turn(4, 1)
+        quantise(1, 1)
         multiply(0, 1)
         multiply(0, 0)
-        square(4)
-        square(2)
-        quantise(1, 1)
         multiply(1, 1)
-        inverse_norm(0)
-        inverse_norm(1)
-        square(3)
-        keys_norm = const.tile([P, 1], F32)
-        nc.vector.reciprocal(out=keys_norm[:], in_=kn_inv[:])
-        beta = const.tile([P, 1], F32)
-        nc.vector.tensor_copy(out=beta[:], in_=beta_bf[:])
-        quantise(2, 1)
-        multiply(2, 1)
-        inverse_norm(2)
-        inverse_den(0)
+        square(2)
         quantise(1, 0)
         multiply(1, 0)
-        quantise(4, 1)
-        multiply(4, 1)
+        quantise(2, 1)
+        multiply(2, 1)
+        square(4, 0)
+        square(4, 1)
+        first_root(0)
+        square(3)
         quantise(2, 0)
         multiply(2, 0)
         quantise(3, 1)
         multiply(3, 1)
-        inverse_norm(4)
-        inverse_norm(3)
-        inverse_den(1)
-        next_table = const.tile([P, 1], F32)
-        nc.scalar.activation(out=next_table[:], in_=inv_den[:, C - 1 : C], func=ACT.Exp)
+        quantise(4, 1)
+        multiply(4, 1)
+        denominator(0)
+        first_root(1)
+        second_root(0)
         quantise(3, 0)
         multiply(3, 0)
+        denominator(1)
+        second_root(1)
+        exp_table()
         quantise(4, 0)
-        inverse(0)
-        score(0)
         multiply(4, 0)
+        score(0)
+        minimum_first()
+        exp_first()
         score(1)
-        score(2)
-        inverse(1)
-
-        nc.vector.tensor_reduce(
-            out=scores[:, C : C + 1], in_=scores[:, 0:SPLIT], axis=AXIS.X, op=ALU.max
-        )
-        score(3)
-        neg_first = const.tile([P, 1], F32)
-        nc.vector.tensor_scalar_mul(out=neg_first[:], in0=scores[:, C : C + 1], scalar1=-1.0)
-        score(4)
-        neg_max = const.tile([P, 1], F32)
-        nc.vector.tensor_reduce(
-            out=neg_max[:], in_=scores[:, SPLIT : C + 1], axis=AXIS.X, op=ALU.max, negate=True
-        )
-        expd = const.tile([P, C], F32)
-        sum_first = const.tile([P, 1], F32)
-        nc.scalar.activation(
-            out=expd[:, 0:SPLIT], in_=scores[:, 0:SPLIT], func=ACT.Exp, bias=neg_first[:], accum_out=sum_first[:]
-        )
-        shift = const.tile([P, 1], F32)
-        nc.scalar.activation(out=shift[:], in_=scores[:, C : C + 1], func=ACT.Exp, bias=neg_max[:])
-        sum_second = const.tile([P, 1], F32)
-        nc.scalar.activation(
-            out=expd[:, SPLIT:C], in_=scores[:, SPLIT:C], func=ACT.Exp, bias=neg_max[:], accum_out=sum_second[:]
-        )
-        total = const.tile([P, 1], F32)
+        minimum_all()
+        exp_shift()
+        exp_second()
         nc.vector.scalar_tensor_tensor(
             out=total[:], in0=sum_first[:], scalar=shift[:, 0:1], in1=sum_second[:], op0=ALU.mult, op1=ALU.add
         )
-        inv_total = const.tile([P, 1], F32)
         nc.vector.reciprocal(out=inv_total[:], in_=total[:])
-        inv_first = const.tile([P, 1], F32)
-        nc.vector.tensor_mul(out=inv_first[:], in0=shift[:], in1=inv_total[:])
         out_rows = out.rearrange("b h c -> (b h) c")
-        left = const.tile([P, SPLIT], F32)
-        nc.vector.tensor_scalar_mul(out=left[:], in0=expd[:, 0:SPLIT], scalar1=inv_first[:, 0:1])
-        nc.sync.dma_start(out=out_rows[:, 0:SPLIT], in_=left[:])
-        right = const.tile([P, C - SPLIT], F32)
-        nc.scalar.activation(
-            out=right[:], in_=expd[:, SPLIT:C], func=ACT.Copy, scale=inv_total[:, 0:1]
-        )
-        nc.scalar.dma_start(out=out_rows[:, SPLIT:C], in_=right[:])
+        for first, second in zip(range(0, SPLIT, PIECE), range(SPLIT, C, PIECE)):
+            cols = slice(first, first + PIECE)
+            nc.vector.tensor_scalar(
+                out=result[:, cols], in0=expd[:, cols], scalar1=shift[:, 0:1], scalar2=inv_total[:, 0:1],
+                op0=ALU.mult, op1=ALU.mult,
+            )
+            nc.sync.dma_start(out=out_rows[:, cols], in_=result[:, cols])
+            cols = slice(second, second + PIECE)
+            nc.scalar.activation(
+                out=result[:, cols], in_=expd[:, cols], func=ACT.Copy, scale=inv_total[:, 0:1]
+            )
+            nc.sync.dma_start(out=out_rows[:, cols], in_=result[:, cols])

@@ -86,9 +86,12 @@ def tile_contentaddressing_s_kernel(tc, memory, keys, betas, mask, out):
         load_mask()
         load_keys()
         load(0, 1)
-        load_both(1)
-        load_both(2)
-        load_both(3)
+        load(1, 0)
+        load(1, 1)
+        load(2, 0)
+        load(2, 1)
+        load(3, 0)
+        load(3, 1)
         load_both(4)
 
         mem_vals = [
@@ -242,8 +245,10 @@ def tile_contentaddressing_s_kernel(tc, memory, keys, betas, mask, out):
         def keys_norm():
             nc.scalar.activation(out=km_sq[:], in_=km[:], func=ACT.Square, accum_out=kn_sq[:])
 
-        def small():
+        def small_kn():
             nc.vector.tensor_scalar_mul(out=kn_scale[:], in0=kn_sq[:], scalar1=2 * EPS)
+
+        def small_beta():
             nc.vector.tensor_scalar_mul(out=beta_neg[:], in0=beta_bf[:], scalar1=-1.0)
 
         def exp_table():
@@ -286,7 +291,6 @@ def tile_contentaddressing_s_kernel(tc, memory, keys, betas, mask, out):
         turn(1, 0)
         turn(1, 1)
         turn_heads(0, km2_bf)
-        keys_norm()
         quantise(0, 0)
         quantise(0, 1)
         turn(2, 0)
@@ -294,7 +298,6 @@ def tile_contentaddressing_s_kernel(tc, memory, keys, betas, mask, out):
         square(1)
         quantise_heads(1)
         quantise_heads(0)
-        small()
         turn(3, 0)
         turn(3, 1)
         turn(4, 0)
@@ -310,6 +313,8 @@ def tile_contentaddressing_s_kernel(tc, memory, keys, betas, mask, out):
         multiply(2, 1)
         square(4, 0)
         square(4, 1)
+        keys_norm()
+        small_beta()
         first_root(0)
         square(3)
         quantise(2, 0)
@@ -318,11 +323,12 @@ def tile_contentaddressing_s_kernel(tc, memory, keys, betas, mask, out):
         multiply(3, 1)
         quantise(4, 1)
         multiply(4, 1)
-        denominator(0)
         first_root(1)
-        second_root(0)
         quantise(3, 0)
         multiply(3, 0)
+        denominator(0)
+        small_kn()
+        second_root(0)
         denominator(1)
         second_root(1)
         exp_table()

@@ -24,6 +24,7 @@ STARTS = [P * sum(TILES[:q]) for q in range(CHUNKS)]
 GROUPS = ((0, 1, 2), (3, 4))
 SCALAR_SQUARES = ((4, 0), (4, 1))
 SPLIT = STARTS[GROUPS[1][0]]
+VECTOR_COPIES = ()
 PIECE = 256
 
 FLOPS = 2 * 2 * B * H * C * W
@@ -103,6 +104,8 @@ def tile_contentaddressing_s_kernel(tc, memory, keys, betas, mask, out):
             for q in range(CHUNKS)
         ]
         codes = {}
+        head_turned = {}
+        mem_turned = {}
         scales = {}
         acc = {}
         m2 = const.tile([P, W], F32)
@@ -137,7 +140,14 @@ def tile_contentaddressing_s_kernel(tc, memory, keys, betas, mask, out):
                     nc.tensor.transpose(
                         turned[:, 2 * t + u, :], words[:, first : first + W // 2 - 1 : 2], ident[:]
                     )
-            nc.scalar.copy(
+            mem_turned[q, b] = turned
+            if (q, b) not in VECTOR_COPIES:
+                place(q, b)
+
+        def place(q, b):
+            turned = mem_turned[q, b]
+            copy = nc.vector.tensor_copy if (q, b) in VECTOR_COPIES else nc.scalar.copy
+            copy(
                 out=mem_vals[q][:, b, :].bitcast(F32).rearrange("p (j m) -> p j m", m=2 * TILES[q]),
                 in_=turned[:].rearrange("p m j -> p j m"),
             )
@@ -147,7 +157,11 @@ def tile_contentaddressing_s_kernel(tc, memory, keys, betas, mask, out):
             turned = psum.tile([P, 2, P], F32, name="bank")
             for u in range(2):
                 nc.tensor.transpose(turned[:, u, :], words[:, u : u + W // 2 - 1 : 2], swap[:])
-            nc.scalar.copy(
+            head_turned[o] = turned
+
+        def place_heads(o, copy):
+            turned = head_turned[o]
+            copy(
                 out=head_vals[:, o, :].bitcast(F32).rearrange("p (r u) -> p r u", u=2),
                 in_=turned[:].rearrange("p u r -> p r u"),
             )
@@ -285,29 +299,31 @@ def tile_contentaddressing_s_kernel(tc, memory, keys, betas, mask, out):
         turn(0, 0)
         turn(0, 1)
         turn_heads(1, m2_bf)
+        place_heads(1, nc.scalar.copy)
         square(0, 0)
         km2_round()
         square(0, 1)
         turn(1, 0)
         turn(1, 1)
-        turn_heads(0, km2_bf)
-        quantise(0, 0)
-        quantise(0, 1)
         turn(2, 0)
         turn(2, 1)
+        turn_heads(0, km2_bf)
+        place_heads(0, nc.scalar.copy)
+        quantise(0, 0)
+        quantise(0, 1)
         square(1)
         quantise_heads(1)
-        quantise_heads(0)
         turn(3, 0)
         turn(3, 1)
         turn(4, 0)
         turn(4, 1)
+        quantise(1, 0)
         quantise(1, 1)
         multiply(0, 1)
-        multiply(0, 0)
         multiply(1, 1)
         square(2)
-        quantise(1, 0)
+        quantise_heads(0)
+        multiply(0, 0)
         multiply(1, 0)
         quantise(2, 1)
         multiply(2, 1)

@@ -22,8 +22,8 @@ TILES = (1, 1, 2, 2, 2)
 CHUNKS = len(TILES)
 STARTS = [P * sum(TILES[:q]) for q in range(CHUNKS)]
 GROUPS = ((0, 1, 2), (3, 4))
-SCALAR_SQUARES = ((4, 0), (4, 1))
-SPLIT = STARTS[GROUPS[1][0]]
+SCALAR_SQUARES = ((4, 0),)
+SPLIT = STARTS[3]
 VECTOR_COPIES = ()
 PIECE = 256
 
@@ -39,10 +39,6 @@ def tile_contentaddressing_s_kernel(tc, memory, keys, betas, mask, out):
         chunk = stack.enter_context(tc.tile_pool(name="chunk", bufs=CHUNKS))
         psum = stack.enter_context(tc.psum_pool(name="psum", bufs=8))
         stack.enter_context(tc.manual_schedule())
-
-        beta_bf = const.tile([P, 1], BF16)
-        with nc.allow_non_contiguous_dma(reason="one beta for each partition, 128 in all"):
-            nc.scalar.dma_start(out=beta_bf[:], in_=betas.rearrange("b (h o) -> (b h) o", o=1))
 
         ident = const.tile([P, P], F32)
         make_identity(nc, ident[:])
@@ -94,6 +90,10 @@ def tile_contentaddressing_s_kernel(tc, memory, keys, betas, mask, out):
         load(3, 0)
         load(3, 1)
         load_both(4)
+
+        beta_bf = const.tile([P, 1], BF16)
+        with nc.allow_non_contiguous_dma(reason="one beta for each partition, 128 in all"):
+            nc.sync.dma_start(out=beta_bf[:], in_=betas.rearrange("b (h o) -> (b h) o", o=1))
 
         mem_vals = [
             chunk.tile([P, B, P * TILES[q] * PACK], BF16, name="mem_vals", align_bytes=64)
@@ -190,6 +190,9 @@ def tile_contentaddressing_s_kernel(tc, memory, keys, betas, mask, out):
                 in_=vals[:].rearrange("p b v -> p (b v)"),
             )
 
+        def group_of(q):
+            return [g for g in range(len(GROUPS)) if q in GROUPS[g]][0]
+
         def group_cells(g):
             return P * sum(TILES[q] for q in GROUPS[g])
 
@@ -198,7 +201,7 @@ def tile_contentaddressing_s_kernel(tc, memory, keys, betas, mask, out):
             return slice(start, start + group_cells(g))
 
         def multiply(q, o):
-            g = [i for i in range(len(GROUPS)) if q in GROUPS[i]][0]
+            g = group_of(q)
             if (g, o) not in acc:
                 acc[g, o] = psum.tile([P, group_cells(g)], F32, name="bank")
             first = STARTS[q] - STARTS[GROUPS[g][0]]
@@ -235,10 +238,13 @@ def tile_contentaddressing_s_kernel(tc, memory, keys, betas, mask, out):
                 scale=kn_scale[:, 0:1], bias=eps_sq[:],
             )
 
-        def score(g):
+        def score(first, stop):
+            g = group_of(first)
+            start = STARTS[GROUPS[g][0]]
+            cols = slice(STARTS[first], STARTS[stop - 1] + P * TILES[stop - 1])
             nc.vector.scalar_tensor_tensor(
-                out=scores[:, group(g)], in0=acc[g, 0][:], scalar=beta_neg[:, 0:1],
-                in1=inv_den[:, group(g)], op0=ALU.mult, op1=ALU.mult,
+                out=scores[:, cols], in0=acc[g, 0][:, cols.start - start : cols.stop - start],
+                scalar=beta_neg[:, 0:1], in1=inv_den[:, cols], op0=ALU.mult, op1=ALU.mult,
             )
 
         def m2_round():
@@ -260,10 +266,10 @@ def tile_contentaddressing_s_kernel(tc, memory, keys, betas, mask, out):
             nc.scalar.activation(out=km_sq[:], in_=km[:], func=ACT.Square, accum_out=kn_sq[:])
 
         def small_kn():
-            nc.vector.tensor_scalar_mul(out=kn_scale[:], in0=kn_sq[:], scalar1=2 * EPS)
+            nc.scalar.activation(out=kn_scale[:], in_=kn_sq[:], func=ACT.Copy, scale=2 * EPS)
 
         def small_beta():
-            nc.vector.tensor_scalar_mul(out=beta_neg[:], in0=beta_bf[:], scalar1=-1.0)
+            nc.scalar.activation(out=beta_neg[:], in_=beta_bf[:], func=ACT.Copy, scale=-1.0)
 
         def exp_table():
             nc.scalar.activation(out=next_table[:], in_=inv_den[:, C - 1 : C], func=ACT.Exp)
@@ -328,32 +334,32 @@ def tile_contentaddressing_s_kernel(tc, memory, keys, betas, mask, out):
         quantise(2, 1)
         multiply(2, 1)
         square(4, 0)
-        square(4, 1)
         keys_norm()
+        small_kn()
         small_beta()
         first_root(0)
         square(3)
-        quantise(2, 0)
-        multiply(2, 0)
+        square(4, 1)
         quantise(3, 1)
         multiply(3, 1)
         quantise(4, 1)
         multiply(4, 1)
         first_root(1)
+        quantise(2, 0)
+        multiply(2, 0)
+        denominator(0)
+        second_root(0)
         quantise(3, 0)
         multiply(3, 0)
-        denominator(0)
-        small_kn()
-        second_root(0)
         denominator(1)
         second_root(1)
         exp_table()
         quantise(4, 0)
         multiply(4, 0)
-        score(0)
+        score(0, 3)
         minimum_first()
         exp_first()
-        score(1)
+        score(3, 5)
         minimum_all()
         exp_shift()
         exp_second()
@@ -362,15 +368,17 @@ def tile_contentaddressing_s_kernel(tc, memory, keys, betas, mask, out):
         )
         nc.vector.reciprocal(out=inv_total[:], in_=total[:])
         out_rows = out.rearrange("b h c -> (b h) c")
-        for first, second in zip(range(0, SPLIT, PIECE), range(SPLIT, C, PIECE)):
+        for first in (0, 512, 256, 768):
             cols = slice(first, first + PIECE)
-            nc.vector.tensor_scalar(
-                out=result[:, cols], in0=expd[:, cols], scalar1=shift[:, 0:1], scalar2=inv_total[:, 0:1],
-                op0=ALU.mult, op1=ALU.mult,
-            )
-            nc.sync.dma_start(out=out_rows[:, cols], in_=result[:, cols])
-            cols = slice(second, second + PIECE)
-            nc.scalar.activation(
-                out=result[:, cols], in_=expd[:, cols], func=ACT.Copy, scale=inv_total[:, 0:1]
-            )
+            if first in (512, 768):
+                nc.scalar.activation(
+                    out=result[:, cols], in_=expd[:, cols], func=ACT.Copy, scale=inv_total[:, 0:1]
+                )
+            elif first < SPLIT:
+                nc.vector.tensor_scalar(
+                    out=result[:, cols], in0=expd[:, cols], scalar1=shift[:, 0:1], scalar2=inv_total[:, 0:1],
+                    op0=ALU.mult, op1=ALU.mult,
+                )
+            else:
+                nc.vector.tensor_scalar_mul(out=result[:, cols], in0=expd[:, cols], scalar1=inv_total[:, 0:1])
             nc.sync.dma_start(out=out_rows[:, cols], in_=result[:, cols])

from contextlib import ExitStack

import concourse.mybir as mybir
from concourse.masks import make_identity

F32 = mybir.dt.float32
BF16 = mybir.dt.bfloat16
U32 = mybir.dt.uint32
U8 = mybir.dt.uint8
FP8X4 = mybir.dt.float8_e4m3fn_x4
ACT = mybir.ActivationFunctionType
ALU = mybir.AluOpType
AXIS = mybir.AxisListType

B, H, C, W = 2, 64, 1024, 512
P = 128
PACK = 4
EPS = 1e-8
GUARD = 1e-26

TILES = (1, 1, 2, 2, 2)
CHUNKS = len(TILES)
STARTS = [P * sum(TILES[:q]) for q in range(CHUNKS)]
GROUPS = ((0, 1, 2), (3, 4))
SCALAR_SQUARES = ((4, 0),)
SPLIT = STARTS[3]
VECTOR_COPIES = ()
PIECE = 256

FLOPS = 2 * 2 * B * H * C * W

assert B * H == P and W == P * PACK and P * sum(TILES) == C


def tile_contentaddressing_s_kernel(tc, memory, keys, betas, mask, out):
    nc = tc.nc
    with ExitStack() as stack:
        const = stack.enter_context(tc.tile_pool(name="const", bufs=1))
        chunk = stack.enter_context(tc.tile_pool(name="chunk", bufs=CHUNKS))
        psum = stack.enter_context(tc.psum_pool(name="psum", bufs=8))
        stack.enter_context(tc.manual_schedule())

        ident = const.tile([P, P], F32)
        make_identity(nc, ident[:])
        swap = const.tile([P, P], F32)
        nc.gpsimd.tensor_copy(out=swap[:, 0:H], in_=ident[:, H:P])
        nc.gpsimd.tensor_copy(out=swap[:, H:P], in_=ident[:, 0:H])
        guard = const.tile([P, 1], F32)
        nc.vector.memset(guard[:], GUARD)
        eps_sq = const.tile([P, 1], F32)
        nc.vector.tensor_scalar(
            out=eps_sq[:], in0=guard[:], scalar1=0.0, scalar2=EPS * EPS, op0=ALU.mult, op1=ALU.add
        )
        first_table = const.tile([P, 1], F32)
        nc.scalar.activation(out=first_table[:], in_=guard[:], func=ACT.Abs_reciprocal_sqrt)

        head_codes = const.tile([P, 7 * H], U32, align_bytes=64)
        head_scales = const.tile([P, 7 * H], U8, align_bytes=64)
        nc.vector.memset(head_codes[:], 0)
        nc.vector.memset(head_scales[:].bitcast(U32), 0)

        mem_view = [
            memory[:, STARTS[q] : STARTS[q] + P * TILES[q], :].rearrange("b (j t) w -> j b (t w)", t=TILES[q])
            for q in range(CHUNKS)
        ]
        cells_sb = [chunk.tile([P, B, TILES[q] * W], BF16, name="cells") for q in range(CHUNKS)]
        mask_sb = const.tile([P, W], BF16)
        keys_sb = const.tile([P, W], BF16)

        def load_mask():
            nc.sync.dma_start(out=mask_sb[:], in_=mask.rearrange("b h w -> (b h) w"))

        def load_keys():
            nc.sync.dma_start(out=keys_sb[:], in_=keys.rearrange("b h w -> (b h) w"))

        def load(q, b):
            nc.sync.dma_start(out=cells_sb[q][:, b, :], in_=mem_view[q][:, b, :])

        def load_both(q):
            nc.sync.dma_start(out=cells_sb[q][:], in_=mem_view[q])

        load(0, 0)
        load_mask()
        load_keys()
        load(0, 1)
        load(1, 0)
        load(1, 1)
        load(2, 0)
        load(2, 1)
        load(3, 0)
        load(3, 1)
        load_both(4)

        beta_bf = const.tile([P, 1], BF16)
        with nc.allow_non_contiguous_dma(reason="one beta for each partition, 128 in all"):
            nc.sync.dma_start(out=beta_bf[:], in_=betas.rearrange("b (h o) -> (b h) o", o=1))

        mem_vals = [
            chunk.tile([P, B, P * TILES[q] * PACK], BF16, name="mem_vals", align_bytes=64)
            for q in range(CHUNKS)
        ]
        sq_vals = [
            chunk.tile([P, B, P * TILES[q] * PACK], BF16, name="sq_vals", align_bytes=64)
            for q in range(CHUNKS)
        ]
        codes = {}
        head_turned = {}
        mem_turned = {}
        scales = {}
        acc = {}
        m2 = const.tile([P, W], F32)
        m2_bf = const.tile([P, W], BF16)
        km = const.tile([P, W], F32)
        km2_bf = const.tile([P, W], BF16)
        km_sq = const.tile([P, W], F32)
        kn_sq = const.tile([P, 1], F32)
        kn_scale = const.tile([P, 1], F32)
        beta_neg = const.tile([P, 1], F32)
        head_vals = const.tile([P, 2, 2 * H * PACK], BF16, align_bytes=64)
        inv_norm = const.tile([P, C], F32)
        den_sq = const.tile([P, C], F32)
        inv_den = const.tile([P, C], F32)
        scores = const.tile([P, C + 1], F32)
        low = const.tile([P, 1], F32)
        next_table = const.tile([P, 1], F32)
        expd = const.tile([P, C], F32)
        sum_first = const.tile([P, 1], F32)
        sum_second = const.tile([P, 1], F32)
        shift = const.tile([P, 1], F32)
        total = const.tile([P, 1], F32)
        inv_total = const.tile([P, 1], F32)
        result = const.tile([P, C], F32)

        def turn(q, b):
            words = cells_sb[q][:, b, :].bitcast(F32)
            turned = psum.tile([P, 2 * TILES[q], P], F32, name="bank")
            for t in range(TILES[q]):
                for u in range(2):
                    first = t * (W // 2) + u
                    nc.tensor.transpose(
                        turned[:, 2 * t + u, :], words[:, first : first + W // 2 - 1 : 2], ident[:]
                    )
            mem_turned[q, b] = turned
            if (q, b) not in VECTOR_COPIES:
                place(q, b)

        def place(q, b):
            turned = mem_turned[q, b]
            copy = nc.vector.tensor_copy if (q, b) in VECTOR_COPIES else nc.scalar.copy
            copy(
                out=mem_vals[q][:, b, :].bitcast(F32).rearrange("p (j m) -> p j m", m=2 * TILES[q]),
                in_=turned[:].rearrange("p m j -> p j m"),
            )

        def turn_heads(o, rows):
            words = rows[:].bitcast(F32)
            turned = psum.tile([P, 2, P], F32, name="bank")
            for u in range(2):
                nc.tensor.transpose(turned[:, u, :], words[:, u : u + W // 2 - 1 : 2], swap[:])
            head_turned[o] = turned

        def place_heads(o, copy):
            turned = head_turned[o]
            copy(
                out=head_vals[:, o, :].bitcast(F32).rearrange("p (r u) -> p r u", u=2),
                in_=turned[:].rearrange("p u r -> p r u"),
            )

        def quantise_heads(o):
            cols = slice(H, 3 * H) if o == 1 else slice(4 * H, 6 * H)
            nc.vector.quantize_mx(
                out=head_codes[:, cols].bitcast(FP8X4), scales=head_scales[:, cols], in_=head_vals[:, o, :]
            )

        def square(q, b=None):
            which = slice(0, B) if b is None else slice(b, b + 1)
            vals = mem_vals[q][:, which, :].rearrange("p b v -> p (b v)")
            squares = sq_vals[q][:, which, :].rearrange("p b v -> p (b v)")
            if b is not None and (q, b) in SCALAR_SQUARES:
                nc.scalar.activation(out=squares, in_=vals, func=ACT.Square)
            else:
                nc.vector.tensor_mul(out=squares, in0=vals, in1=vals)

        def quantise(q, o):
            codes[q, o] = chunk.tile([P, B * P * TILES[q]], U32, name="codes%d" % o, align_bytes=64)
            scales[q, o] = chunk.tile([P, B * P * TILES[q]], U8, name="scales%d" % o, align_bytes=64)
            vals = sq_vals[q] if o == 1 else mem_vals[q]
            nc.vector.quantize_mx(
                out=codes[q, o][:].bitcast(FP8X4), scales=scales[q, o][:],
                in_=vals[:].rearrange("p b v -> p (b v)"),
            )

        def group_of(q):
            return [g for g in range(len(GROUPS)) if q in GROUPS[g]][0]

        def group_cells(g):
            return P * sum(TILES[q] for q in GROUPS[g])

        def group(g):
            start = STARTS[GROUPS[g][0]]
            return slice(start, start + group_cells(g))

        def multiply(q, o):
            g = group_of(q)
            if (g, o) not in acc:
                acc[g, o] = psum.tile([P, group_cells(g)], F32, name="bank")
            first = STARTS[q] - STARTS[GROUPS[g][0]]
            cells = P * TILES[q]
            base = 0 if o == 1 else 3 * H
            for b in range(B):
                heads = slice(base + 2 * H * (1 - b), base + 2 * H * (1 - b) + P)
                cols = slice(b * cells, (b + 1) * cells)
                nc.tensor.matmul_mx(
                    out=acc[g, o][:, first : first + cells],
                    lhsT=head_codes[:, heads].bitcast(FP8X4),
                    lhsT_scale=head_scales[:, heads],
                    rhs=codes[q, o][:, cols].bitcast(FP8X4),
                    rhs_scale=scales[q, o][:, cols],
                    start=(b == 0),
                    stop=(b == B - 1),
                )

        def first_root(g):
            nc.scalar.activation(
                out=inv_norm[:, group(g)], in_=acc[g, 1][:], func=ACT.Abs_reciprocal_sqrt,
                scale=kn_sq[:, 0:1], bias=guard[:],
            )

        def denominator(g):
            nc.vector.scalar_tensor_tensor(
                out=den_sq[:, group(g)], in0=inv_norm[:, group(g)], scalar=1 / (2 * EPS),
                in1=acc[g, 1][:], op0=ALU.add, op1=ALU.mult,
            )

        def second_root(g):
            nc.scalar.activation(
                out=inv_den[:, group(g)], in_=den_sq[:, group(g)], func=ACT.Abs_reciprocal_sqrt,
                scale=kn_scale[:, 0:1], bias=eps_sq[:],
            )

        def score(first, stop):
            g = group_of(first)
            start = STARTS[GROUPS[g][0]]
            cols = slice(STARTS[first], STARTS[stop - 1] + P * TILES[stop - 1])
            nc.vector.scalar_tensor_tensor(
                out=scores[:, cols], in0=acc[g, 0][:, cols.start - start : cols.stop - start],
                scalar=beta_neg[:, 0:1], in1=inv_den[:, cols], op0=ALU.mult, op1=ALU.mult,
            )

        def m2_round():
            nc.vector.tensor_mul(out=m2_bf[:], in0=mask_sb[:], in1=mask_sb[:])

        def m2_scalar():
            nc.scalar.activation(out=m2[:], in_=mask_sb[:], func=ACT.Square)

        def m2_vector():
            nc.vector.tensor_mul(out=m2[:], in0=mask_sb[:], in1=mask_sb[:])

        def km2_round():
            nc.vector.tensor_mul(out=km2_bf[:], in0=keys_sb[:], in1=m2[:])

        def km_make():
            nc.vector.tensor_mul(out=km[:], in0=keys_sb[:], in1=mask_sb[:])

        def keys_norm():
            nc.scalar.activation(out=km_sq[:], in_=km[:], func=ACT.Square, accum_out=kn_sq[:])

        def small_kn():
            nc.scalar.activation(out=kn_scale[:], in_=kn_sq[:], func=ACT.Copy, scale=2 * EPS)

        def small_beta():
            nc.scalar.activation(out=beta_neg[:], in_=beta_bf[:], func=ACT.Copy, scale=-1.0)

        def exp_table():
            nc.scalar.activation(out=next_table[:], in_=inv_den[:, C - 1 : C], func=ACT.Exp)

        def minimum_first():
            nc.vector.tensor_reduce(
                out=scores[:, C : C + 1], in_=scores[:, 0:SPLIT], axis=AXIS.X, op=ALU.min
            )

        def minimum_all():
            nc.vector.tensor_reduce(out=low[:], in_=scores[:, SPLIT : C + 1], axis=AXIS.X, op=ALU.min)

        def exp_first():
            nc.scalar.activation(
                out=expd[:, 0:SPLIT], in_=scores[:, 0:SPLIT], func=ACT.Exp, scale=-1.0,
                bias=scores[:, C : C + 1], accum_out=sum_first[:],
            )

        def exp_shift():
            nc.scalar.activation(
                out=shift[:], in_=scores[:, C : C + 1], func=ACT.Exp, scale=-1.0, bias=low[:]
            )

        def exp_second():
            nc.scalar.activation(
                out=expd[:, SPLIT:C], in_=scores[:, SPLIT:C], func=ACT.Exp, scale=-1.0,
                bias=low[:], accum_out=sum_second[:],
            )

        m2_round()
        m2_scalar()
        km_make()
        turn(0, 0)
        turn(0, 1)
        turn_heads(1, m2_bf)
        place_heads(1, nc.scalar.copy)
        square(0, 0)
        km2_round()
        square(0, 1)
        turn(1, 0)
        turn(1, 1)
        turn(2, 0)
        turn(2, 1)
        turn_heads(0, km2_bf)
        place_heads(0, nc.scalar.copy)
        quantise(0, 0)
        quantise(0, 1)
        square(1)
        quantise_heads(1)
        turn(3, 0)
        turn(3, 1)
        turn(4, 0)
        turn(4, 1)
        quantise(1, 0)
        quantise(1, 1)
        multiply(0, 1)
        multiply(1, 1)
        square(2)
        quantise_heads(0)
        multiply(0, 0)
        multiply(1, 0)
        quantise(2, 1)
        multiply(2, 1)
        square(4, 0)
        keys_norm()
        small_kn()
        small_beta()
        first_root(0)
        square(3)
        square(4, 1)
        quantise(3, 1)
        multiply(3, 1)
        quantise(4, 1)
        multiply(4, 1)
        first_root(1)
        quantise(2, 0)
        multiply(2, 0)
        denominator(0)
        second_root(0)
        quantise(3, 0)
        multiply(3, 0)
        denominator(1)
        second_root(1)
        exp_table()
        quantise(4, 0)
        multiply(4, 0)
        score(0, 3)
        minimum_first()
        exp_first()
        score(3, 5)
        minimum_all()
        exp_shift()
        exp_second()
        nc.vector.scalar_tensor_tensor(
            out=total[:], in0=sum_first[:], scalar=shift[:, 0:1], in1=sum_second[:], op0=ALU.mult, op1=ALU.add
        )
        nc.vector.reciprocal(out=inv_total[:], in_=total[:])
        out_rows = out.rearrange("b h c -> (b h) c")
        for first in (0, 512, 256, 768):
            cols = slice(first, first + PIECE)
            if first in (512, 768):
                nc.scalar.activation(
                    out=result[:, cols], in_=expd[:, cols], func=ACT.Copy, scale=inv_total[:, 0:1]
                )
            elif first < SPLIT:
                nc.vector.tensor_scalar(
                    out=result[:, cols], in0=expd[:, cols], scalar1=shift[:, 0:1], scalar2=inv_total[:, 0:1],
                    op0=ALU.mult, op1=ALU.mult,
                )
            else:
                nc.vector.tensor_scalar_mul(out=result[:, cols], in0=expd[:, cols], scalar1=inv_total[:, 0:1])
            nc.sync.dma_start(out=out_rows[:, cols], in_=result[:, cols])
